import numpy as np
import ml_dtypes


def mxq(x, axis, fmt="e4m3"):
    dtype, down = {"e4m3": (ml_dtypes.float8_e4m3fn, 7), "e5m2": (ml_dtypes.float8_e5m2, 14)}[fmt]
    v = np.moveaxis(np.asarray(x, np.float32).astype(ml_dtypes.bfloat16).astype(np.float64), axis, -1)
    blocks = v.reshape(v.shape[:-1] + (-1, 32))
    amax = np.abs(blocks).max(-1, keepdims=True)
    byte = np.maximum(np.where(amax > 0, np.frexp(amax)[1] - 1 + 127, 0) - down, 1)
    scale = np.exp2(byte - 127.0)
    codes = (blocks / scale).astype(np.float32).astype(dtype).astype(np.float64)
    return np.moveaxis((codes * scale).reshape(v.shape), -1, axis)


WIDE = False


def mx_kscale(k):
    if not WIDE:
        return np.ones(k)
    levels = np.array([10, -10, 5, -5, 0])
    a = np.random.permutation(np.resize(levels, k // 512 * 4)).reshape(k // 512, 4)
    idx = np.arange(k)
    return np.exp2(a[idx // 512, idx % 128 // 32])


BF16 = ml_dtypes.bfloat16


def bf(x):
    return np.asarray(x, np.float32).astype(BF16)


def f64(x):
    return np.asarray(x).astype(np.float64)


E2M1 = np.array([0.0, 0.5, 1.0, 1.5, 2.0, 3.0, 4.0, 6.0, -0.0, -0.5, -1.0, -1.5, -2.0, -3.0, -4.0, -6.0])


def pack_weight(w, fmt):
    k, n = w.shape
    w = f64(bf(w)).reshape(k // 32, 32, n)
    amax = np.abs(w).max(1)
    if fmt == "e4m3":
        byte = np.frexp(amax)[1] - 1 + 127 - 7
    else:
        mant, ex = np.frexp(amax / 6.0)
        byte = np.where(mant > 0.5, ex, ex - 1) + 127
    byte = np.clip(np.where(amax > 0, byte, 1), 1, 254)
    scaled = (w * np.exp2(127.0 - byte)[:, None, :]).reshape(k, n).astype(np.float32)
    by_word = np.ascontiguousarray(scaled.reshape(k // 512, 128, 4, n).transpose(0, 1, 3, 2))
    if fmt == "e4m3":
        words = by_word.astype(ml_dtypes.float8_e4m3fn).view(np.uint8)
    else:
        c = by_word.astype(ml_dtypes.float4_e2m1fn).view(np.uint8) & 0xF
        words = c[..., 0::2] | (c[..., 1::2] << 4)
    return np.ascontiguousarray(words), np.ascontiguousarray(byte.astype(np.uint8).reshape(k // 512, 16, n))


def unpack_weight(words, scales, fmt):
    g, p, n, _ = words.shape
    if fmt == "e4m3":
        vals = np.ascontiguousarray(words).view(ml_dtypes.float8_e4m3fn).astype(np.float64)
    else:
        nib = np.empty((g, p, n, 4), np.uint8)
        nib[..., 0::2] = words & 0xF
        nib[..., 1::2] = words >> 4
        vals = E2M1[nib]
    vals = vals * np.repeat(np.exp2(scales.astype(np.float64) - 127.0), 8, axis=1)[..., None]
    return vals.transpose(0, 1, 3, 2).reshape(g * 512, n)


B, T, E, Q = 4, 512, 1024, 512
N = B * T


def setup_inputs():
    s = mx_kscale(Q)
    y = bf(np.random.standard_normal((B, T, Q)) * s)
    w = np.random.standard_normal((2 * E, Q)) / np.sqrt(Q) / s
    words, scales = pack_weight(np.ascontiguousarray(w.T), "e4m3")
    return {"y": y, "w_swiglu_words": words, "w_swiglu_scales": scales}


def reference(y, w_swiglu_words, w_swiglu_scales):
    uv = mxq(f64(y).reshape(N, Q), 1, "e4m3") @ unpack_weight(w_swiglu_words, w_swiglu_scales, "e4m3")
    u, v = uv[:, :E], uv[:, E:]
    ao = mxq(u.T, 1, "e4m3") @ mxq(v, 0, "e4m3")
    return ao / B * E ** (-0.5)

@@ -1,0 +1,164 @@
+import math
+from contextlib import ExitStack
+
+import concourse.mybir as mybir
+from concourse.masks import make_identity
+
+F32 = mybir.dt.float32
+BF16 = mybir.dt.bfloat16
+I32 = mybir.dt.int32
+U32 = mybir.dt.uint32
+U8 = mybir.dt.uint8
+FP8X4 = mybir.dt.float8_e4m3fn_x4
+
+P = 128
+PACK = 4
+K_PASS = P * PACK
+TOKENS = 2048
+FEATURES = 512
+E = 1024
+GROUPS = TOKENS // K_PASS
+D_TILES = E // P
+N_WIDE = 512
+E_CHUNKS = E // N_WIDE
+QUAD = 4
+PAIR_WORDS = FEATURES // 2
+OUT_SCALE = 1.0 / (4.0 * math.sqrt(1024.0))
+
+FLOPS = 2 * TOKENS * FEATURES * 2 * E + 2 * E * TOKENS * E
+
+
+def tile_retentionmechanism_pa_kernel(tc, y, w_swiglu_words, w_swiglu_scales, out):
+    nc = tc.nc
+    with ExitStack() as ctx:
+        keep = ctx.enter_context(tc.tile_pool(name="keep", bufs=1))
+        stage = ctx.enter_context(tc.tile_pool(name="stage", bufs=3))
+        results = ctx.enter_context(tc.tile_pool(name="results", bufs=4))
+        psum = ctx.enter_context(tc.psum_pool(name="psum", bufs=4))
+        ctx.enter_context(tc.manual_schedule())
+
+        y_sb = keep.tile([P, GROUPS, PACK, FEATURES], BF16)
+        w_codes = keep.tile([P, 2 * E], U32, align_bytes=64)
+        w_scales = keep.tile([P, 2 * E], U8, align_bytes=64)
+        y_codes = keep.tile([P, GROUPS, PACK, P], U32, align_bytes=64)
+        y_scales = keep.tile([P, GROUPS, PACK, P], U8, align_bytes=64)
+        v_codes = keep.tile([P, GROUPS, E], U32, align_bytes=64)
+        v_scales = keep.tile([P, GROUPS, E], U8, align_bytes=64)
+        u_codes = keep.tile([P, D_TILES, GROUPS, P], U32, align_bytes=64)
+        u_scales = keep.tile([P, D_TILES, GROUPS, P], U8, align_bytes=64)
+        ident = keep.tile([P, P], F32)
+
+        nc.vector.memset(w_scales[:].bitcast(I32), 0)
+        make_identity(nc, ident[:])
+
+        def load_y(g):
+            nc.sync.dma_start(out=y_sb[:, g], in_=y[g].rearrange("(p j) q -> p j q", j=PACK))
+
+        def load_w_codes(first, count):
+            words = w_swiglu_words[0].rearrange("p n t -> p (n t)").bitcast(I32)
+            nc.sync.dma_start(
+                out=w_codes[:, first : first + count].bitcast(I32), in_=words[:, first : first + count]
+            )
+
+        load_y(0)
+        load_y(1)
+        for r in range(4):
+            nc.sync.dma_start(
+                out=w_scales[r:P:32, :].bitcast(I32), in_=w_swiglu_scales[0, r:16:4, :].bitcast(I32)
+            )
+        load_w_codes(E, E)
+        load_y(2)
+        load_y(3)
+        load_w_codes(0, E)
+
+        def quantise(filled):
+            grouped, codes, scales = filled
+            nc.vector.quantize_mx(
+                out=codes.bitcast(FP8X4), scales=scales, in_=grouped[:].rearrange("p a b j -> p (a b j)")
+            )
+
+        def transpose_y(g):
+            grouped = stage.tile([P, PACK, P, PACK], BF16, tag="grouped", align_bytes=64)
+            grouped_pairs = grouped[:].bitcast(F32)
+            for half in range(2):
+                bank = psum.tile([P, 2, 2, P], F32, tag="wide")
+                for i in range(2):
+                    y_pairs = y_sb[:, g, 2 * half + i, :].bitcast(F32)
+                    for pair in range(2):
+                        nc.tensor.transpose(bank[:, i, pair, :], y_pairs[:, pair:PAIR_WORDS:2], ident[:])
+                copy = nc.vector.tensor_copy if half == 0 else nc.scalar.copy
+                copy(
+                    out=grouped_pairs[:, 2 * half : 2 * half + 2],
+                    in_=bank[:].rearrange("p i pair n -> p i n pair"),
+                )
+            return (
+                grouped,
+                y_codes[:, g].rearrange("p j n -> p (j n)"),
+                y_scales[:, g].rearrange("p j n -> p (j n)"),
+            )
+
+        def project(pieces):
+            grouped = stage.tile([P, QUAD, P, PACK], BF16, tag="grouped", align_bytes=64)
+            for i, (g, first) in enumerate(pieces):
+                bank = psum.tile([P, PACK, P], F32, tag="uv")
+                for j in range(PACK):
+                    nc.tensor.matmul_mx(
+                        out=bank[:, j, :],
+                        lhsT=y_codes[:, g, j, :].bitcast(FP8X4),
+                        lhsT_scale=y_scales[:, g, j, :],
+                        rhs=w_codes[:, first : first + P].bitcast(FP8X4),
+                        rhs_scale=w_scales[:, first : first + P],
+                        start=True,
+                        stop=True,
+                    )
+                copy = nc.vector.tensor_copy if i == 1 else nc.scalar.copy
+                copy(out=grouped[:, i], in_=bank[:].rearrange("p j c -> p c j"))
+            return grouped
+
+        def contract(d):
+            for chunk in range(E_CHUNKS):
+                cols = slice(chunk * N_WIDE, (chunk + 1) * N_WIDE)
+                acc = psum.tile([P, N_WIDE], F32, tag="wide")
+                for g in range(GROUPS):
+                    nc.tensor.matmul_mx(
+                        out=acc[:],
+                        lhsT=u_codes[:, d, g, :].bitcast(FP8X4),
+                        lhsT_scale=u_scales[:, d, g, :],
+                        rhs=v_codes[:, g, cols].bitcast(FP8X4),
+                        rhs_scale=v_scales[:, g, cols],
+                        start=(g == 0),
+                        stop=(g == GROUPS - 1),
+                    )
+                result = results.tile([P, N_WIDE], F32)
+                if chunk == 0:
+                    nc.vector.tensor_scalar_mul(out=result[:], in0=acc[:], scalar1=OUT_SCALE)
+                else:
+                    nc.scalar.mul(out=result[:], in_=acc[:], mul=OUT_SCALE)
+                nc.sync.dma_start(out=out[d * P : (d + 1) * P, cols], in_=result[:])
+
+        quantise(transpose_y(0))
+        filled = transpose_y(1)
+
+        for g in range(GROUPS):
+            for chunk in range(E_CHUNKS):
+                first = chunk * N_WIDE
+                grouped = project([(g, E + first + i * P) for i in range(QUAD)])
+                quantise(filled)
+                filled = (grouped, v_codes[:, g, first : first + N_WIDE], v_scales[:, g, first : first + N_WIDE])
+            if g + 2 < GROUPS:
+                newer = transpose_y(g + 2)
+                quantise(filled)
+                filled = newer
+
+        for d in range(D_TILES):
+            grouped = project([(g, d * P) for g in range(GROUPS)])
+            quantise(filled)
+            filled = (
+                grouped,
+                u_codes[:, d].rearrange("p g c -> p (g c)"),
+                u_scales[:, d].rearrange("p g c -> p (g c)"),
+            )
+            if d > 0:
+                contract(d - 1)
+        quantise(filled)
+        contract(D_TILES - 1)

@@ -78,18 +78,24 @@ def tile_retentionmechanism_pa_kernel(tc, y, w_swiglu_words, w_swiglu_scales, ou
             )
 
         def transpose_y(g):
-            grouped = stage.tile([P, PACK, P, PACK], BF16, tag="grouped", align_bytes=64)
-            grouped_pairs = grouped[:].bitcast(F32)
+            banks = []
             for half in range(2):
                 bank = psum.tile([P, 2, 2, P], F32, tag="wide")
                 for i in range(2):
                     y_pairs = y_sb[:, g, 2 * half + i, :].bitcast(F32)
                     for pair in range(2):
                         nc.tensor.transpose(bank[:, i, pair, :], y_pairs[:, pair:PAIR_WORDS:2], ident[:])
+                banks.append(bank)
+            return banks
+
+        def regroup_y(g, banks):
+            grouped = stage.tile([P, PACK, P, PACK], BF16, tag="grouped", align_bytes=64)
+            grouped_pairs = grouped[:].bitcast(F32)
+            for half in range(2):
                 copy = nc.vector.tensor_copy if half == 0 else nc.scalar.copy
                 copy(
                     out=grouped_pairs[:, 2 * half : 2 * half + 2],
-                    in_=bank[:].rearrange("p i pair n -> p i n pair"),
+                    in_=banks[half][:].rearrange("p i pair n -> p i n pair"),
                 )
             return (
                 grouped,
@@ -136,29 +142,37 @@ def tile_retentionmechanism_pa_kernel(tc, y, w_swiglu_words, w_swiglu_scales, ou
                     nc.scalar.mul(out=result[:], in_=acc[:], mul=OUT_SCALE)
                 nc.sync.dma_start(out=out[d * P : (d + 1) * P, cols], in_=result[:])
 
-        quantise(transpose_y(0))
-        filled = transpose_y(1)
+        def project_v(g, chunk):
+            first = chunk * N_WIDE
+            grouped = project([(g, E + first + i * P) for i in range(QUAD)])
+            return (grouped, v_codes[:, g, first : first + N_WIDE], v_scales[:, g, first : first + N_WIDE])
 
-        for g in range(GROUPS):
-            for chunk in range(E_CHUNKS):
-                first = chunk * N_WIDE
-                grouped = project([(g, E + first + i * P) for i in range(QUAD)])
-                quantise(filled)
-                filled = (grouped, v_codes[:, g, first : first + N_WIDE], v_scales[:, g, first : first + N_WIDE])
-            if g + 2 < GROUPS:
-                newer = transpose_y(g + 2)
-                quantise(filled)
-                filled = newer
-
-        for d in range(D_TILES):
+        def project_u(d):
             grouped = project([(g, d * P) for g in range(GROUPS)])
-            quantise(filled)
-            filled = (
+            return (
                 grouped,
                 u_codes[:, d].rearrange("p g c -> p (g c)"),
                 u_scales[:, d].rearrange("p g c -> p (g c)"),
             )
-            if d > 0:
-                contract(d - 1)
+
+        def quantise_older(older, newer):
+            quantise(older)
+            return newer
+
+        quantise(regroup_y(0, transpose_y(0)))
+        filled = regroup_y(1, transpose_y(1))
+
+        for g in range(GROUPS):
+            filled = quantise_older(filled, project_v(g, 0))
+            if g + 2 < GROUPS:
+                banks = transpose_y(g + 2)
+            filled = quantise_older(filled, project_v(g, 1))
+            if g + 2 < GROUPS:
+                filled = quantise_older(filled, regroup_y(g + 2, banks))
+
+        filled = quantise_older(filled, project_u(0))
         quantise(filled)
-        contract(D_TILES - 1)
+        for d in range(D_TILES):
+            if d + 1 < D_TILES:
+                quantise(project_u(d + 1))
+            contract(d)

@@ -20,7 +20,6 @@ E = 1024
 GROUPS = TOKENS // K_PASS
 D_TILES = E // P
 N_WIDE = 512
-E_CHUNKS = E // N_WIDE
 QUAD = 4
 PAIR_WORDS = FEATURES // 2
 OUT_SCALE = 1.0 / (4.0 * math.sqrt(1024.0))
@@ -34,7 +33,7 @@ def tile_retentionmechanism_pa_kernel(tc, y, w_swiglu_words, w_swiglu_scales, ou
         keep = ctx.enter_context(tc.tile_pool(name="keep", bufs=1))
         stage = ctx.enter_context(tc.tile_pool(name="stage", bufs=3))
         results = ctx.enter_context(tc.tile_pool(name="results", bufs=4))
-        psum = ctx.enter_context(tc.psum_pool(name="psum", bufs=4))
+        psum = ctx.enter_context(tc.psum_pool(name="psum", bufs=8))
         ctx.enter_context(tc.manual_schedule())
 
         y_sb = keep.tile([P, GROUPS, PACK, FEATURES], BF16)
@@ -80,7 +79,7 @@ def tile_retentionmechanism_pa_kernel(tc, y, w_swiglu_words, w_swiglu_scales, ou
         def transpose_y(g):
             banks = []
             for half in range(2):
-                bank = psum.tile([P, 2, 2, P], F32, tag="wide")
+                bank = psum.tile([P, 2, 2, P], F32, tag="bank")
                 for i in range(2):
                     y_pairs = y_sb[:, g, 2 * half + i, :].bitcast(F32)
                     for pair in range(2):
@@ -106,7 +105,7 @@ def tile_retentionmechanism_pa_kernel(tc, y, w_swiglu_words, w_swiglu_scales, ou
         def project(pieces):
             grouped = stage.tile([P, QUAD, P, PACK], BF16, tag="grouped", align_bytes=64)
             for i, (g, first) in enumerate(pieces):
-                bank = psum.tile([P, PACK, P], F32, tag="uv")
+                bank = psum.tile([P, PACK, P], F32, tag="bank")
                 for j in range(PACK):
                     nc.tensor.matmul_mx(
                         out=bank[:, j, :],
@@ -121,26 +120,25 @@ def tile_retentionmechanism_pa_kernel(tc, y, w_swiglu_words, w_swiglu_scales, ou
                 copy(out=grouped[:, i], in_=bank[:].rearrange("p j c -> p c j"))
             return grouped
 
-        def contract(d):
-            for chunk in range(E_CHUNKS):
-                cols = slice(chunk * N_WIDE, (chunk + 1) * N_WIDE)
-                acc = psum.tile([P, N_WIDE], F32, tag="wide")
-                for g in range(GROUPS):
-                    nc.tensor.matmul_mx(
-                        out=acc[:],
-                        lhsT=u_codes[:, d, g, :].bitcast(FP8X4),
-                        lhsT_scale=u_scales[:, d, g, :],
-                        rhs=v_codes[:, g, cols].bitcast(FP8X4),
-                        rhs_scale=v_scales[:, g, cols],
-                        start=(g == 0),
-                        stop=(g == GROUPS - 1),
-                    )
-                result = results.tile([P, N_WIDE], F32)
-                if chunk == 0:
-                    nc.vector.tensor_scalar_mul(out=result[:], in0=acc[:], scalar1=OUT_SCALE)
-                else:
-                    nc.scalar.mul(out=result[:], in_=acc[:], mul=OUT_SCALE)
-                nc.sync.dma_start(out=out[d * P : (d + 1) * P, cols], in_=result[:])
+        def contract(d, chunk):
+            cols = slice(chunk * N_WIDE, (chunk + 1) * N_WIDE)
+            acc = psum.tile([P, N_WIDE], F32, tag="bank")
+            for g in range(GROUPS):
+                nc.tensor.matmul_mx(
+                    out=acc[:],
+                    lhsT=u_codes[:, d, g, :].bitcast(FP8X4),
+                    lhsT_scale=u_scales[:, d, g, :],
+                    rhs=v_codes[:, g, cols].bitcast(FP8X4),
+                    rhs_scale=v_scales[:, g, cols],
+                    start=(g == 0),
+                    stop=(g == GROUPS - 1),
+                )
+            result = results.tile([P, N_WIDE], F32)
+            if chunk == 0:
+                nc.vector.tensor_scalar_mul(out=result[:], in0=acc[:], scalar1=OUT_SCALE)
+            else:
+                nc.scalar.mul(out=result[:], in_=acc[:], mul=OUT_SCALE)
+            nc.sync.dma_start(out=out[d * P : (d + 1) * P, cols], in_=result[:])
 
         def project_v(g, chunk):
             first = chunk * N_WIDE
@@ -165,14 +163,16 @@ def tile_retentionmechanism_pa_kernel(tc, y, w_swiglu_words, w_swiglu_scales, ou
         for g in range(GROUPS):
             filled = quantise_older(filled, project_v(g, 0))
             if g + 2 < GROUPS:
-                banks = transpose_y(g + 2)
-            filled = quantise_older(filled, project_v(g, 1))
-            if g + 2 < GROUPS:
-                filled = quantise_older(filled, regroup_y(g + 2, banks))
+                filled = quantise_older(filled, regroup_y(g + 2, transpose_y(g + 2)))
 
         filled = quantise_older(filled, project_u(0))
         quantise(filled)
         for d in range(D_TILES):
             if d + 1 < D_TILES:
                 quantise(project_u(d + 1))
-            contract(d)
+            if d < GROUPS:
+                quantise(project_v(d, 1))
+            contract(d, 0)
+
+        for d in range(D_TILES):
+            contract(d, 1)

@@ -21,6 +21,7 @@ GROUPS = TOKENS // K_PASS
 D_TILES = E // P
 N_WIDE = 512
 QUAD = 4
+HALF = PACK // 2
 PAIR_WORDS = FEATURES // 2
 OUT_SCALE = 1.0 / (4.0 * math.sqrt(1024.0))
 
@@ -31,10 +32,10 @@ def tile_retentionmechanism_pa_kernel(tc, y, w_swiglu_words, w_swiglu_scales, ou
     nc = tc.nc
     with ExitStack() as ctx:
         keep = ctx.enter_context(tc.tile_pool(name="keep", bufs=1))
-        stage = ctx.enter_context(tc.tile_pool(name="stage", bufs=3))
+        y_stage = ctx.enter_context(tc.tile_pool(name="y_stage", bufs=4))
+        uv_stage = ctx.enter_context(tc.tile_pool(name="uv_stage", bufs=3))
         results = ctx.enter_context(tc.tile_pool(name="results", bufs=4))
         psum = ctx.enter_context(tc.psum_pool(name="psum", bufs=8))
-        ctx.enter_context(tc.manual_schedule())
 
         y_sb = keep.tile([P, GROUPS, PACK, FEATURES], BF16)
         w_codes = keep.tile([P, 2 * E], U32, align_bytes=64)
@@ -50,8 +51,8 @@ def tile_retentionmechanism_pa_kernel(tc, y, w_swiglu_words, w_swiglu_scales, ou
         nc.vector.memset(w_scales[:].bitcast(I32), 0)
         make_identity(nc, ident[:])
 
-        def load_y(g):
-            nc.sync.dma_start(out=y_sb[:, g], in_=y[g].rearrange("(p j) q -> p j q", j=PACK))
+        def load_y(g, tiles):
+            nc.sync.dma_start(out=y_sb[:, g, tiles], in_=y[g].rearrange("(p j) q -> p j q", j=PACK)[:, tiles])
 
         def load_w_codes(first, count):
             words = w_swiglu_words[0].rearrange("p n t -> p (n t)").bitcast(I32)
@@ -59,51 +60,36 @@ def tile_retentionmechanism_pa_kernel(tc, y, w_swiglu_words, w_swiglu_scales, ou
                 out=w_codes[:, first : first + count].bitcast(I32), in_=words[:, first : first + count]
             )
 
-        load_y(0)
-        load_y(1)
+        load_y(0, slice(0, HALF))
+        load_y(0, slice(HALF, PACK))
+        load_y(1, slice(0, PACK))
         for r in range(4):
             nc.sync.dma_start(
                 out=w_scales[r:P:32, :].bitcast(I32), in_=w_swiglu_scales[0, r:16:4, :].bitcast(I32)
             )
         load_w_codes(E, E)
-        load_y(2)
-        load_y(3)
+        load_y(2, slice(0, PACK))
+        load_y(3, slice(0, PACK))
         load_w_codes(0, E)
 
-        def quantise(filled):
-            grouped, codes, scales = filled
-            nc.vector.quantize_mx(
-                out=codes.bitcast(FP8X4), scales=scales, in_=grouped[:].rearrange("p a b j -> p (a b j)")
-            )
-
-        def transpose_y(g):
-            banks = []
-            for half in range(2):
-                bank = psum.tile([P, 2, 2, P], F32, tag="bank")
-                for i in range(2):
-                    y_pairs = y_sb[:, g, 2 * half + i, :].bitcast(F32)
+        def quantise_y(g):
+            for first in range(0, PACK, HALF):
+                tiles = slice(first, first + HALF)
+                bank = psum.tile([P, HALF, 2, P], F32, tag="bank")
+                for i in range(HALF):
+                    y_pairs = y_sb[:, g, first + i, :].bitcast(F32)
                     for pair in range(2):
                         nc.tensor.transpose(bank[:, i, pair, :], y_pairs[:, pair:PAIR_WORDS:2], ident[:])
-                banks.append(bank)
-            return banks
-
-        def regroup_y(g, banks):
-            grouped = stage.tile([P, PACK, P, PACK], BF16, tag="grouped", align_bytes=64)
-            grouped_pairs = grouped[:].bitcast(F32)
-            for half in range(2):
-                copy = nc.vector.tensor_copy if half == 0 else nc.scalar.copy
-                copy(
-                    out=grouped_pairs[:, 2 * half : 2 * half + 2],
-                    in_=banks[half][:].rearrange("p i pair n -> p i n pair"),
+                grouped = y_stage.tile([P, HALF, P, PACK], BF16, align_bytes=64)
+                nc.scalar.copy(out=grouped[:].bitcast(F32), in_=bank[:].rearrange("p i pair n -> p i n pair"))
+                nc.vector.quantize_mx(
+                    out=y_codes[:, g, tiles].rearrange("p i n -> p (i n)").bitcast(FP8X4),
+                    scales=y_scales[:, g, tiles].rearrange("p i n -> p (i n)"),
+                    in_=grouped[:].rearrange("p i n j -> p (i n j)"),
                 )
-            return (
-                grouped,
-                y_codes[:, g].rearrange("p j n -> p (j n)"),
-                y_scales[:, g].rearrange("p j n -> p (j n)"),
-            )
 
-        def project(pieces):
-            grouped = stage.tile([P, QUAD, P, PACK], BF16, tag="grouped", align_bytes=64)
+        def project(pieces, vector_banks, codes, scales):
+            grouped = uv_stage.tile([P, QUAD, P, PACK], BF16, align_bytes=64)
             for i, (g, first) in enumerate(pieces):
                 bank = psum.tile([P, PACK, P], F32, tag="bank")
                 for j in range(PACK):
@@ -116,13 +102,28 @@ def tile_retentionmechanism_pa_kernel(tc, y, w_swiglu_words, w_swiglu_scales, ou
                         start=True,
                         stop=True,
                     )
-                copy = nc.vector.tensor_copy if i == 1 else nc.scalar.copy
+                copy = nc.vector.tensor_copy if i in vector_banks else nc.scalar.copy
                 copy(out=grouped[:, i], in_=bank[:].rearrange("p j c -> p c j"))
-            return grouped
+            nc.vector.quantize_mx(
+                out=codes.bitcast(FP8X4), scales=scales, in_=grouped[:].rearrange("p i c j -> p (i c j)")
+            )
 
-        def contract(d, chunk):
+        def project_v(g, chunk):
             cols = slice(chunk * N_WIDE, (chunk + 1) * N_WIDE)
-            acc = psum.tile([P, N_WIDE], F32, tag="bank")
+            pieces = [(g, E + chunk * N_WIDE + i * P) for i in range(QUAD)]
+            project(pieces, (1, 3), v_codes[:, g, cols], v_scales[:, g, cols])
+
+        def project_u(d):
+            project(
+                [(g, d * P) for g in range(GROUPS)],
+                (1,),
+                u_codes[:, d].rearrange("p g c -> p (g c)"),
+                u_scales[:, d].rearrange("p g c -> p (g c)"),
+            )
+
+        def contract(d, first, width, scale_on_vector):
+            cols = slice(first, first + width)
+            acc = psum.tile([P, width], F32, tag="bank")
             for g in range(GROUPS):
                 nc.tensor.matmul_mx(
                     out=acc[:],
@@ -133,46 +134,33 @@ def tile_retentionmechanism_pa_kernel(tc, y, w_swiglu_words, w_swiglu_scales, ou
                     start=(g == 0),
                     stop=(g == GROUPS - 1),
                 )
-            result = results.tile([P, N_WIDE], F32)
-            if chunk == 0:
+            result = results.tile([P, width], F32, tag="result")
+            if scale_on_vector:
                 nc.vector.tensor_scalar_mul(out=result[:], in0=acc[:], scalar1=OUT_SCALE)
             else:
                 nc.scalar.mul(out=result[:], in_=acc[:], mul=OUT_SCALE)
             nc.sync.dma_start(out=out[d * P : (d + 1) * P, cols], in_=result[:])
 
-        def project_v(g, chunk):
-            first = chunk * N_WIDE
-            grouped = project([(g, E + first + i * P) for i in range(QUAD)])
-            return (grouped, v_codes[:, g, first : first + N_WIDE], v_scales[:, g, first : first + N_WIDE])
 
-        def project_u(d):
-            grouped = project([(g, d * P) for g in range(GROUPS)])
-            return (
-                grouped,
-                u_codes[:, d].rearrange("p g c -> p (g c)"),
-                u_scales[:, d].rearrange("p g c -> p (g c)"),
-            )
+        quantise_y(0)
+        quantise_y(1)
+        project_v(0, 0)
+        quantise_y(2)
+        quantise_y(3)
+        for g in range(1, GROUPS):
+            project_v(g, 0)
+        project_u(0)
 
-        def quantise_older(older, newer):
-            quantise(older)
-            return newer
-
-        quantise(regroup_y(0, transpose_y(0)))
-        filled = regroup_y(1, transpose_y(1))
-
-        for g in range(GROUPS):
-            filled = quantise_older(filled, project_v(g, 0))
-            if g + 2 < GROUPS:
-                filled = quantise_older(filled, regroup_y(g + 2, transpose_y(g + 2)))
-
-        filled = quantise_older(filled, project_u(0))
-        quantise(filled)
         for d in range(D_TILES):
             if d + 1 < D_TILES:
-                quantise(project_u(d + 1))
+                project_u(d + 1)
             if d < GROUPS:
-                quantise(project_v(d, 1))
-            contract(d, 0)
+                project_v(d, 1)
+            contract(d, 0, N_WIDE, True)
+            if d >= GROUPS:
+                contract(d - GROUPS, N_WIDE, N_WIDE, False)
 
-        for d in range(D_TILES):
-            contract(d, 1)
+        for d in range(GROUPS, D_TILES - 1):
+            contract(d, N_WIDE, N_WIDE, d % 2 == 0)
+        contract(D_TILES - 1, N_WIDE, N_WIDE // 2, False)
+        contract(D_TILES - 1, N_WIDE + N_WIDE // 2, N_WIDE // 2, True)

@@ -23,6 +23,7 @@ N_WIDE = 512
 QUAD = 4
 HALF = PACK // 2
 PAIR_WORDS = FEATURES // 2
+WARM_UP = 4
 OUT_SCALE = 1.0 / (4.0 * math.sqrt(1024.0))
 
 FLOPS = 2 * TOKENS * FEATURES * 2 * E + 2 * E * TOKENS * E
@@ -47,9 +48,18 @@ def tile_retentionmechanism_pa_kernel(tc, y, w_swiglu_words, w_swiglu_scales, ou
         u_codes = keep.tile([P, D_TILES, GROUPS, P], U32, align_bytes=64)
         u_scales = keep.tile([P, D_TILES, GROUPS, P], U8, align_bytes=64)
         ident = keep.tile([P, P], F32)
+        warm = keep.tile([P, N_WIDE], BF16)
 
+        nc.vector.memset(warm[:], 0.0)
         nc.vector.memset(w_scales[:].bitcast(I32), 0)
         make_identity(nc, ident[:])
+
+        def idle_matmul(stationary, moving):
+            scratch = psum.tile([P, N_WIDE], F32, tag="bank")
+            nc.tensor.matmul(out=scratch[:], lhsT=stationary, rhs=moving, start=True, stop=True)
+
+        for i in range(WARM_UP):
+            idle_matmul(warm[:, 0:P], warm[:])
 
         def load_y(g, tiles):
             nc.sync.dma_start(out=y_sb[:, g, tiles], in_=y[g].rearrange("(p j) q -> p j q", j=PACK)[:, tiles])
@@ -80,6 +90,8 @@ def tile_retentionmechanism_pa_kernel(tc, y, w_swiglu_words, w_swiglu_scales, ou
                     y_pairs = y_sb[:, g, first + i, :].bitcast(F32)
                     for pair in range(2):
                         nc.tensor.transpose(bank[:, i, pair, :], y_pairs[:, pair:PAIR_WORDS:2], ident[:])
+                if g < 2:
+                    idle_matmul(y_sb[:, g, first, 0:P], y_sb[:, g, first, :])
                 grouped = y_stage.tile([P, HALF, P, PACK], BF16, align_bytes=64)
                 nc.scalar.copy(out=grouped[:].bitcast(F32), in_=bank[:].rearrange("p i pair n -> p i n pair"))
                 nc.vector.quantize_mx(

@@ -72,15 +72,17 @@ def tile_retentionmechanism_pa_kernel(tc, y, w_swiglu_words, w_swiglu_scales, ou
 
         load_y(0, slice(0, HALF))
         load_y(0, slice(HALF, PACK))
-        load_y(1, slice(0, PACK))
+        load_y(1, slice(0, HALF))
+        load_y(1, slice(HALF, PACK))
         for r in range(4):
             nc.sync.dma_start(
                 out=w_scales[r:P:32, :].bitcast(I32), in_=w_swiglu_scales[0, r:16:4, :].bitcast(I32)
             )
-        load_w_codes(E, E)
+        load_w_codes(E, N_WIDE)
         load_y(2, slice(0, PACK))
         load_y(3, slice(0, PACK))
         load_w_codes(0, E)
+        load_w_codes(E + N_WIDE, N_WIDE)
 
         def quantise_y(g):
             for first in range(0, PACK, HALF):
@@ -90,7 +92,7 @@ def tile_retentionmechanism_pa_kernel(tc, y, w_swiglu_words, w_swiglu_scales, ou
                     y_pairs = y_sb[:, g, first + i, :].bitcast(F32)
                     for pair in range(2):
                         nc.tensor.transpose(bank[:, i, pair, :], y_pairs[:, pair:PAIR_WORDS:2], ident[:])
-                if g < 2:
+                if (g, first) in ((0, HALF), (1, 0)):
                     idle_matmul(y_sb[:, g, first, 0:P], y_sb[:, g, first, :])
                 grouped = y_stage.tile([P, HALF, P, PACK], BF16, align_bytes=64)
                 nc.scalar.copy(out=grouped[:].bitcast(F32), in_=bank[:].rearrange("p i pair n -> p i n pair"))
@@ -157,10 +159,11 @@ def tile_retentionmechanism_pa_kernel(tc, y, w_swiglu_words, w_swiglu_scales, ou
         quantise_y(0)
         quantise_y(1)
         project_v(0, 0)
+        project_v(1, 0)
         quantise_y(2)
         quantise_y(3)
-        for g in range(1, GROUPS):
-            project_v(g, 0)
+        project_v(2, 0)
+        project_v(3, 0)
         project_u(0)
 
         for d in range(D_TILES):

@@ -35,7 +35,7 @@ def tile_retentionmechanism_pa_kernel(tc, y, w_swiglu_words, w_swiglu_scales, ou
         keep = ctx.enter_context(tc.tile_pool(name="keep", bufs=1))
         y_stage = ctx.enter_context(tc.tile_pool(name="y_stage", bufs=4))
         uv_stage = ctx.enter_context(tc.tile_pool(name="uv_stage", bufs=3))
-        results = ctx.enter_context(tc.tile_pool(name="results", bufs=4))
+        results = ctx.enter_context(tc.tile_pool(name="results", bufs=8))
         psum = ctx.enter_context(tc.psum_pool(name="psum", bufs=8))
 
         y_sb = keep.tile([P, GROUPS, PACK, FEATURES], BF16)
@@ -70,18 +70,24 @@ def tile_retentionmechanism_pa_kernel(tc, y, w_swiglu_words, w_swiglu_scales, ou
                 out=w_codes[:, first : first + count].bitcast(I32), in_=words[:, first : first + count]
             )
 
+        def load_w_scales(first, count):
+            for r in range(4):
+                nc.sync.dma_start(
+                    out=w_scales[r:P:32, first : first + count].bitcast(I32),
+                    in_=w_swiglu_scales[0, r:16:4, first : first + count].bitcast(I32),
+                )
+
         load_y(0, slice(0, HALF))
+        load_w_scales(E, N_WIDE)
         load_y(0, slice(HALF, PACK))
         load_y(1, slice(0, HALF))
         load_y(1, slice(HALF, PACK))
-        for r in range(4):
-            nc.sync.dma_start(
-                out=w_scales[r:P:32, :].bitcast(I32), in_=w_swiglu_scales[0, r:16:4, :].bitcast(I32)
-            )
         load_w_codes(E, N_WIDE)
         load_y(2, slice(0, PACK))
         load_y(3, slice(0, PACK))
+        load_w_scales(0, E)
         load_w_codes(0, E)
+        load_w_scales(E + N_WIDE, N_WIDE)
         load_w_codes(E + N_WIDE, N_WIDE)
 
         def quantise_y(g):
@@ -178,4 +184,5 @@ def tile_retentionmechanism_pa_kernel(tc, y, w_swiglu_words, w_swiglu_scales, ou
         for d in range(GROUPS, D_TILES - 1):
             contract(d, N_WIDE, N_WIDE, d % 2 == 0)
         contract(D_TILES - 1, N_WIDE, N_WIDE // 2, False)
-        contract(D_TILES - 1, N_WIDE + N_WIDE // 2, N_WIDE // 2, True)
+        contract(D_TILES - 1, N_WIDE + N_WIDE // 2, P, True)
+        contract(D_TILES - 1, E - P, P, True)

@@ -165,9 +165,9 @@ def tile_retentionmechanism_pa_kernel(tc, y, w_swiglu_words, w_swiglu_scales, ou
         quantise_y(0)
         quantise_y(1)
         project_v(0, 0)
-        project_v(1, 0)
         quantise_y(2)
         quantise_y(3)
+        project_v(1, 0)
         project_v(2, 0)
         project_v(3, 0)
         project_u(0)

@@ -175,13 +175,11 @@ def tile_retentionmechanism_pa_kernel(tc, y, w_swiglu_words, w_swiglu_scales, ou
         for d in range(D_TILES):
             if d + 1 < D_TILES:
                 project_u(d + 1)
-            if d < GROUPS:
-                project_v(d, 1)
-            contract(d, 0, N_WIDE, True)
-            if d >= GROUPS:
-                contract(d - GROUPS, N_WIDE, N_WIDE, False)
+            if d % 2 == 0:
+                project_v(d // 2, 1)
+            contract(d, 0, N_WIDE, d % 2 == 0)
 
-        for d in range(GROUPS, D_TILES - 1):
+        for d in range(D_TILES - 1):
             contract(d, N_WIDE, N_WIDE, d % 2 == 0)
         contract(D_TILES - 1, N_WIDE, N_WIDE // 2, False)
         contract(D_TILES - 1, N_WIDE + N_WIDE // 2, P, True)

@@ -37,6 +37,7 @@ def tile_retentionmechanism_pa_kernel(tc, y, w_swiglu_words, w_swiglu_scales, ou
         uv_stage = ctx.enter_context(tc.tile_pool(name="uv_stage", bufs=3))
         results = ctx.enter_context(tc.tile_pool(name="results", bufs=8))
         psum = ctx.enter_context(tc.psum_pool(name="psum", bufs=8))
+        ctx.enter_context(tc.manual_schedule(engines={mybir.EngineType.PE}))
 
         y_sb = keep.tile([P, GROUPS, PACK, FEATURES], BF16)
         w_codes = keep.tile([P, 2 * E], U32, align_bytes=64)

import math
from contextlib import ExitStack

import concourse.mybir as mybir
from concourse.masks import make_identity

F32 = mybir.dt.float32
BF16 = mybir.dt.bfloat16
I32 = mybir.dt.int32
U32 = mybir.dt.uint32
U8 = mybir.dt.uint8
FP8X4 = mybir.dt.float8_e4m3fn_x4

P = 128
PACK = 4
K_PASS = P * PACK
TOKENS = 2048
FEATURES = 512
E = 1024
GROUPS = TOKENS // K_PASS
D_TILES = E // P
N_WIDE = 512
QUAD = 4
HALF = PACK // 2
PAIR_WORDS = FEATURES // 2
WARM_UP = 4
OUT_SCALE = 1.0 / (4.0 * math.sqrt(1024.0))

FLOPS = 2 * TOKENS * FEATURES * 2 * E + 2 * E * TOKENS * E


def tile_retentionmechanism_pa_kernel(tc, y, w_swiglu_words, w_swiglu_scales, out):
    nc = tc.nc
    with ExitStack() as ctx:
        keep = ctx.enter_context(tc.tile_pool(name="keep", bufs=1))
        y_stage = ctx.enter_context(tc.tile_pool(name="y_stage", bufs=4))
        uv_stage = ctx.enter_context(tc.tile_pool(name="uv_stage", bufs=3))
        results = ctx.enter_context(tc.tile_pool(name="results", bufs=8))
        psum = ctx.enter_context(tc.psum_pool(name="psum", bufs=8))
        ctx.enter_context(tc.manual_schedule(engines={mybir.EngineType.PE}))

        y_sb = keep.tile([P, GROUPS, PACK, FEATURES], BF16)
        w_codes = keep.tile([P, 2 * E], U32, align_bytes=64)
        w_scales = keep.tile([P, 2 * E], U8, align_bytes=64)
        y_codes = keep.tile([P, GROUPS, PACK, P], U32, align_bytes=64)
        y_scales = keep.tile([P, GROUPS, PACK, P], U8, align_bytes=64)
        v_codes = keep.tile([P, GROUPS, E], U32, align_bytes=64)
        v_scales = keep.tile([P, GROUPS, E], U8, align_bytes=64)
        u_codes = keep.tile([P, D_TILES, GROUPS, P], U32, align_bytes=64)
        u_scales = keep.tile([P, D_TILES, GROUPS, P], U8, align_bytes=64)
        ident = keep.tile([P, P], F32)
        warm = keep.tile([P, N_WIDE], BF16)

        nc.vector.memset(warm[:], 0.0)
        nc.vector.memset(w_scales[:].bitcast(I32), 0)
        make_identity(nc, ident[:])

        def idle_matmul(stationary, moving):
            scratch = psum.tile([P, N_WIDE], F32, tag="bank")
            nc.tensor.matmul(out=scratch[:], lhsT=stationary, rhs=moving, start=True, stop=True)

        for i in range(WARM_UP):
            idle_matmul(warm[:, 0:P], warm[:])

        def load_y(g, tiles):
            nc.sync.dma_start(out=y_sb[:, g, tiles], in_=y[g].rearrange("(p j) q -> p j q", j=PACK)[:, tiles])

        def load_w_codes(first, count):
            words = w_swiglu_words[0].rearrange("p n t -> p (n t)").bitcast(I32)
            nc.sync.dma_start(
                out=w_codes[:, first : first + count].bitcast(I32), in_=words[:, first : first + count]
            )

        def load_w_scales(first, count):
            for r in range(4):
                nc.sync.dma_start(
                    out=w_scales[r:P:32, first : first + count].bitcast(I32),
                    in_=w_swiglu_scales[0, r:16:4, first : first + count].bitcast(I32),
                )

        load_y(0, slice(0, HALF))
        load_w_scales(E, N_WIDE)
        load_y(0, slice(HALF, PACK))
        load_y(1, slice(0, HALF))
        load_y(1, slice(HALF, PACK))
        load_w_codes(E, N_WIDE)
        load_y(2, slice(0, PACK))
        load_y(3, slice(0, PACK))
        load_w_scales(0, E)
        load_w_codes(0, E)
        load_w_scales(E + N_WIDE, N_WIDE)
        load_w_codes(E + N_WIDE, N_WIDE)

        def quantise_y(g):
            for first in range(0, PACK, HALF):
                tiles = slice(first, first + HALF)
                bank = psum.tile([P, HALF, 2, P], F32, tag="bank")
                for i in range(HALF):
                    y_pairs = y_sb[:, g, first + i, :].bitcast(F32)
                    for pair in range(2):
                        nc.tensor.transpose(bank[:, i, pair, :], y_pairs[:, pair:PAIR_WORDS:2], ident[:])
                if (g, first) in ((0, HALF), (1, 0)):
                    idle_matmul(y_sb[:, g, first, 0:P], y_sb[:, g, first, :])
                grouped = y_stage.tile([P, HALF, P, PACK], BF16, align_bytes=64)
                nc.scalar.copy(out=grouped[:].bitcast(F32), in_=bank[:].rearrange("p i pair n -> p i n pair"))
                nc.vector.quantize_mx(
                    out=y_codes[:, g, tiles].rearrange("p i n -> p (i n)").bitcast(FP8X4),
                    scales=y_scales[:, g, tiles].rearrange("p i n -> p (i n)"),
                    in_=grouped[:].rearrange("p i n j -> p (i n j)"),
                )

        def project(pieces, vector_banks, codes, scales):
            grouped = uv_stage.tile([P, QUAD, P, PACK], BF16, align_bytes=64)
            for i, (g, first) in enumerate(pieces):
                bank = psum.tile([P, PACK, P], F32, tag="bank")
                for j in range(PACK):
                    nc.tensor.matmul_mx(
                        out=bank[:, j, :],
                        lhsT=y_codes[:, g, j, :].bitcast(FP8X4),
                        lhsT_scale=y_scales[:, g, j, :],
                        rhs=w_codes[:, first : first + P].bitcast(FP8X4),
                        rhs_scale=w_scales[:, first : first + P],
                        start=True,
                        stop=True,
                    )
                copy = nc.vector.tensor_copy if i in vector_banks else nc.scalar.copy
                copy(out=grouped[:, i], in_=bank[:].rearrange("p j c -> p c j"))
            nc.vector.quantize_mx(
                out=codes.bitcast(FP8X4), scales=scales, in_=grouped[:].rearrange("p i c j -> p (i c j)")
            )

        def project_v(g, chunk):
            cols = slice(chunk * N_WIDE, (chunk + 1) * N_WIDE)
            pieces = [(g, E + chunk * N_WIDE + i * P) for i in range(QUAD)]
            project(pieces, (1, 3), v_codes[:, g, cols], v_scales[:, g, cols])

        def project_u(d):
            project(
                [(g, d * P) for g in range(GROUPS)],
                (1,),
                u_codes[:, d].rearrange("p g c -> p (g c)"),
                u_scales[:, d].rearrange("p g c -> p (g c)"),
            )

        def contract(d, first, width, scale_on_vector):
            cols = slice(first, first + width)
            acc = psum.tile([P, width], F32, tag="bank")
            for g in range(GROUPS):
                nc.tensor.matmul_mx(
                    out=acc[:],
                    lhsT=u_codes[:, d, g, :].bitcast(FP8X4),
                    lhsT_scale=u_scales[:, d, g, :],
                    rhs=v_codes[:, g, cols].bitcast(FP8X4),
                    rhs_scale=v_scales[:, g, cols],
                    start=(g == 0),
                    stop=(g == GROUPS - 1),
                )
            result = results.tile([P, width], F32, tag="result")
            if scale_on_vector:
                nc.vector.tensor_scalar_mul(out=result[:], in0=acc[:], scalar1=OUT_SCALE)
            else:
                nc.scalar.mul(out=result[:], in_=acc[:], mul=OUT_SCALE)
            nc.sync.dma_start(out=out[d * P : (d + 1) * P, cols], in_=result[:])


        quantise_y(0)
        quantise_y(1)
        project_v(0, 0)
        quantise_y(2)
        quantise_y(3)
        project_v(1, 0)
        project_v(2, 0)
        project_v(3, 0)
        project_u(0)

        for d in range(D_TILES):
            if d + 1 < D_TILES:
                project_u(d + 1)
            if d % 2 == 0:
                project_v(d // 2, 1)
            contract(d, 0, N_WIDE, d % 2 == 0)

        for d in range(D_TILES - 1):
            contract(d, N_WIDE, N_WIDE, d % 2 == 0)
        contract(D_TILES - 1, N_WIDE, N_WIDE // 2, False)
        contract(D_TILES - 1, N_WIDE + N_WIDE // 2, P, True)
        contract(D_TILES - 1, E - P, P, True)
